import numpy as np
import ml_dtypes


def mxq(x, axis, fmt="e4m3"):
    dtype, down = {"e4m3": (ml_dtypes.float8_e4m3fn, 7), "e5m2": (ml_dtypes.float8_e5m2, 14)}[fmt]
    v = np.moveaxis(np.asarray(x, np.float32).astype(ml_dtypes.bfloat16).astype(np.float64), axis, -1)
    blocks = v.reshape(v.shape[:-1] + (-1, 32))
    amax = np.abs(blocks).max(-1, keepdims=True)
    byte = np.maximum(np.where(amax > 0, np.frexp(amax)[1] - 1 + 127, 0) - down, 1)
    scale = np.exp2(byte - 127.0)
    codes = (blocks / scale).astype(np.float32).astype(dtype).astype(np.float64)
    return np.moveaxis((codes * scale).reshape(v.shape), -1, axis)


WIDE = False


def mx_kscale(k):
    if not WIDE:
        return np.ones(k)
    levels = np.array([10, -10, 5, -5, 0])
    a = np.random.permutation(np.resize(levels, k // 512 * 4)).reshape(k // 512, 4)
    idx = np.arange(k)
    return np.exp2(a[idx // 512, idx % 128 // 32])


BF16 = ml_dtypes.bfloat16


def bf(x):
    return np.asarray(x, np.float32).astype(BF16)


def f64(x):
    return np.asarray(x).astype(np.float64)


B, C, RR, O, H, W = 2, 512, 16, 128, 16, 16
N = H * W
E0 = 7.0
YS = np.sqrt(E0 / N)
PEAK = 1.8


def setup_inputs():
    u = mx_kscale(C + C)
    t, s = u[:C], u[C:]
    logits = PEAK * np.random.standard_normal((B, C, C))
    p = np.exp(logits - logits.max(-1, keepdims=True))
    attention = p / p.sum(-1, keepdims=True)
    wz = np.random.standard_normal((O, C)) * 0.6 / (YS * np.sqrt(C)) / t
    wx = np.random.standard_normal((O, C)) * 0.7 / np.sqrt(C) / s
    return {"attention": bf(attention * t[:, None] / t[None, :]),
            "v": bf(YS * np.random.standard_normal((B, C, N)) * t[:, None]),
            "x": bf(np.random.standard_normal((B, C, N)) * s[:, None]),
            "wf": bf(np.concatenate([wz, wx], axis=1)),
            "b_fuse": bf(0.2 * np.random.standard_normal(O)),
            "gamma": bf(2.0 + 0.2 * np.random.standard_normal(1))}


def reference(attention, v, x, wf, b_fuse, gamma):
    v = f64(v)
    mixed = mxq(f64(attention), 2, "e4m3") @ mxq(v, 1, "e4m3")
    z = f64(gamma) * mixed + v
    cat = np.concatenate([z, f64(x)], axis=1)
    fused = mxq(f64(wf), 1, "e4m3") @ mxq(cat, 1, "e4m3")
    return fused + f64(b_fuse)[None, :, None]

@@ -1,0 +1,199 @@
+from contextlib import ExitStack
+
+import concourse.masks as masks
+import concourse.mybir as mybir
+
+BF16 = mybir.dt.bfloat16
+F32 = mybir.dt.float32
+U32 = mybir.dt.uint32
+U8 = mybir.dt.uint8
+FP8X4 = mybir.dt.float8_e4m3fn_x4
+ALU = mybir.AluOpType
+ACT = mybir.ActivationFunctionType
+
+P = 128
+PACK = 4
+K_PASS = P * PACK
+PAIR = 2
+
+IMAGES = 2
+CHANNELS = 512
+POSITIONS = 256
+OUT_CHANNELS = 128
+HALVES = POSITIONS // P
+
+FLOPS = 2 * IMAGES * POSITIONS * (CHANNELS * CHANNELS + OUT_CHANNELS * 2 * CHANNELS)
+
+
+def flip_k_last(nc, banks, ident, rows):
+    words = rows[:].bitcast(F32).rearrange("r (s p u) -> r s u p", s=2, u=PAIR)
+    flipped = banks.tile([P, 2, PAIR, P], F32, name="flipped")
+    for s in range(2):
+        for u in range(PAIR):
+            nc.tensor.transpose(flipped[:, s, u, :], words[:, s, u, :], ident[:])
+    return flipped
+
+
+def leave_psum(nc, keep, flipped, label):
+    grouped = keep.tile([P, 2 * P * PACK], BF16, align_bytes=64, name="grouped_" + label)
+    nc.scalar.copy(
+        out=grouped[:].bitcast(F32).rearrange("p (s r u) -> p s r u", s=2, u=PAIR),
+        in_=flipped[:].rearrange("p s u r -> p s r u"),
+    )
+    return grouped
+
+
+def regroup_k_first(copy, keep, rows, label):
+    grouped = keep.tile([P, POSITIONS * PACK], BF16, align_bytes=64, name="grouped_" + label)
+    copy(
+        out=grouped[:].rearrange("p (c i j) -> p c j i", i=4, j=PACK),
+        in_=rows[:].rearrange("p j (c i) -> p c j i", i=4),
+    )
+    return grouped
+
+
+def quantise(nc, keep, grouped, label):
+    codes = keep.tile([P, POSITIONS], U32, align_bytes=64, name="codes_" + label)
+    scales = keep.tile([P, POSITIONS], U8, align_bytes=64, name="scales_" + label)
+    nc.vector.quantize_mx(out=codes[:].bitcast(FP8X4), scales=scales[:], in_=grouped[:])
+    return codes, scales
+
+
+def multiply(nc, acc, weights, w_cols, moving, n_cols, start, stop):
+    nc.tensor.matmul_mx(
+        out=acc,
+        lhsT=weights[0][:, w_cols].bitcast(FP8X4),
+        lhsT_scale=weights[1][:, w_cols],
+        rhs=moving[0][:, n_cols].bitcast(FP8X4),
+        rhs_scale=moving[1][:, n_cols],
+        start=start,
+        stop=stop,
+    )
+
+
+def tile_gcam_pb_s_kernel(tc, attention, v, x, wf, b_fuse, gamma, out):
+    nc = tc.nc
+    with ExitStack() as ctx:
+        keep = ctx.enter_context(tc.tile_pool(name="keep", bufs=1))
+        banks = ctx.enter_context(tc.psum_pool(name="banks", bufs=3))
+        mixed_banks = ctx.enter_context(tc.psum_pool(name="mixed_banks", bufs=3))
+        fused_banks = ctx.enter_context(tc.psum_pool(name="fused_banks", bufs=2))
+        ctx.enter_context(tc.manual_schedule())
+
+        gamma_bf = keep.tile([P, 1], BF16, name="gamma_bf")
+        nc.scalar.dma_start(out=gamma_bf[:], in_=gamma.partition_broadcast(P))
+        bias_bf = keep.tile([P, 1], BF16, name="bias_bf")
+        nc.scalar.dma_start(out=bias_bf[:], in_=b_fuse.rearrange("(o one) -> o one", one=1))
+
+        att_rows = attention.rearrange("b (m t) d -> b m t d", t=PACK)
+        v_rows = v.rearrange("b (p j) n -> b p j n", j=PACK)
+        x_rows = x.rearrange("b (p j) n -> b p j n", j=PACK)
+        att_sb = {}
+        v_sb = {}
+        x_sb = {}
+        for b in range(IMAGES):
+            for s in range(2):
+                att_sb[b, s] = keep.tile([P, 2 * CHANNELS], BF16, name="att_sb_%d%d" % (b, s))
+                nc.sync.dma_start(
+                    out=att_sb[b, s][:].rearrange("m (t d) -> m t d", t=2),
+                    in_=att_rows[b, :, 2 * s : 2 * s + 2, :],
+                )
+            v_sb[b] = keep.tile([P, PACK, POSITIONS], BF16, name="v_sb_%d" % b)
+            nc.sync.dma_start(out=v_sb[b][:], in_=v_rows[b])
+        wf_sb = keep.tile([P, 2 * CHANNELS], BF16, name="wf_sb")
+        nc.sync.dma_start(out=wf_sb[:], in_=wf)
+        for b in range(IMAGES):
+            x_sb[b] = keep.tile([P, PACK, POSITIONS], BF16, name="x_sb_%d" % b)
+            nc.sync.dma_start(out=x_sb[b][:], in_=x_rows[b])
+
+        ident = keep.tile([P, P], F32, name="ident")
+        masks.make_identity(nc, ident[:])
+        gamma_f32 = keep.tile([P, 1], F32, name="gamma_f32")
+        nc.gpsimd.tensor_copy(out=gamma_f32[:], in_=gamma_bf[:])
+        bias_f32 = keep.tile([P, 1], F32, name="bias_f32")
+        nc.gpsimd.tensor_copy(out=bias_f32[:], in_=bias_bf[:])
+        table_warm = keep.tile([P, 1], F32, name="table_warm")
+        nc.scalar.activation(out=table_warm[:], in_=ident[:, 0:1], func=ACT.Identity)
+
+        att_grouped = {}
+        att_mx = {}
+        v_grouped = {}
+        v_mx = {}
+        mixed = {}
+        z_grouped = {}
+        z_mx = {}
+        x_grouped = {}
+        x_mx = {}
+        fused = {}
+
+        def flip_attention(b):
+            for s in range(2):
+                flipped = flip_k_last(nc, banks, ident, att_sb[b, s])
+                att_grouped[b, s] = leave_psum(nc, keep, flipped, "att_%d%d" % (b, s))
+
+        def quantise_stage_1(b):
+            v_grouped[b] = regroup_k_first(nc.vector.tensor_copy, keep, v_sb[b], "v_%d" % b)
+            att_mx[b, 0] = quantise(nc, keep, att_grouped[b, 0], "att_%d0" % b)
+            v_mx[b] = quantise(nc, keep, v_grouped[b], "v_%d" % b)
+            att_mx[b, 1] = quantise(nc, keep, att_grouped[b, 1], "att_%d1" % b)
+
+        def mix(b):
+            for h in range(HALVES):
+                mixed[b, h] = mixed_banks.tile([P, PACK, P], F32, name="mixed")
+                for t in range(PACK):
+                    multiply(
+                        nc,
+                        mixed[b, h][:, t, :],
+                        att_mx[b, t // 2],
+                        slice((t % 2) * P, (t % 2 + 1) * P),
+                        v_mx[b],
+                        slice(h * P, (h + 1) * P),
+                        True,
+                        True,
+                    )
+
+        def add_v(b):
+            z_grouped[b] = keep.tile([P, POSITIONS * PACK], BF16, align_bytes=64, name="z_grouped_%d" % b)
+            for h in range(HALVES):
+                cols = slice(h * P * PACK, (h + 1) * P * PACK)
+                nc.vector.scalar_tensor_tensor(
+                    out=z_grouped[b][:, cols].rearrange("m (n t) -> m n t", t=PACK),
+                    in0=mixed[b, h][:].rearrange("m t n -> m n t"),
+                    scalar=gamma_f32[:, 0:1],
+                    in1=v_grouped[b][:, cols].rearrange("m (n t) -> m n t", t=PACK),
+                    op0=ALU.mult,
+                    op1=ALU.add,
+                )
+
+        def fuse(b):
+            every = slice(0, POSITIONS)
+            fused[b] = fused_banks.tile([P, POSITIONS], F32, name="fused")
+            multiply(nc, fused[b][:], wf_mx, slice(P, 2 * P), x_mx[b], every, True, False)
+            multiply(nc, fused[b][:], wf_mx, slice(0, P), z_mx[b], every, False, True)
+
+        def add_bias_and_store(b):
+            result = keep.tile([P, POSITIONS], F32, name="result_%d" % b)
+            nc.scalar.activation(out=result[:], in_=fused[b][:], func=ACT.Identity, bias=bias_f32[:, 0:1])
+            nc.sync.dma_start(out=out[b], in_=result[:])
+
+        flip_attention(0)
+        quantise_stage_1(0)
+        flip_attention(1)
+        mix(0)
+        quantise_stage_1(1)
+        wf_flipped = flip_k_last(nc, banks, ident, wf_sb)
+        mix(1)
+        x_grouped[0] = regroup_k_first(nc.scalar.copy, keep, x_sb[0], "x_0")
+        wf_grouped = leave_psum(nc, keep, wf_flipped, "wf")
+        x_grouped[1] = regroup_k_first(nc.scalar.copy, keep, x_sb[1], "x_1")
+        add_v(0)
+        x_mx[0] = quantise(nc, keep, x_grouped[0], "x_0")
+        z_mx[0] = quantise(nc, keep, z_grouped[0], "z_0")
+        wf_mx = quantise(nc, keep, wf_grouped, "wf")
+        fuse(0)
+        add_v(1)
+        x_mx[1] = quantise(nc, keep, x_grouped[1], "x_1")
+        z_mx[1] = quantise(nc, keep, z_grouped[1], "z_1")
+        add_bias_and_store(0)
+        fuse(1)
+        add_bias_and_store(1)

@@ -21,6 +21,8 @@ CHANNELS = 512
 POSITIONS = 256
 OUT_CHANNELS = 128
 HALVES = POSITIONS // P
+ONES_ROW = 32
+SPREAD_COLS = 32
 
 FLOPS = 2 * IMAGES * POSITIONS * (CHANNELS * CHANNELS + OUT_CHANNELS * 2 * CHANNELS)
 
@@ -75,15 +77,23 @@ def tile_gcam_pb_s_kernel(tc, attention, v, x, wf, b_fuse, gamma, out):
     nc = tc.nc
     with ExitStack() as ctx:
         keep = ctx.enter_context(tc.tile_pool(name="keep", bufs=1))
-        banks = ctx.enter_context(tc.psum_pool(name="banks", bufs=3))
+        banks = ctx.enter_context(tc.psum_pool(name="banks", bufs=2))
         mixed_banks = ctx.enter_context(tc.psum_pool(name="mixed_banks", bufs=3))
         fused_banks = ctx.enter_context(tc.psum_pool(name="fused_banks", bufs=2))
+        small_bank = ctx.enter_context(tc.psum_pool(name="small_bank", bufs=1))
         ctx.enter_context(tc.manual_schedule())
 
-        gamma_bf = keep.tile([P, 1], BF16, name="gamma_bf")
-        nc.scalar.dma_start(out=gamma_bf[:], in_=gamma.partition_broadcast(P))
-        bias_bf = keep.tile([P, 1], BF16, name="bias_bf")
-        nc.scalar.dma_start(out=bias_bf[:], in_=b_fuse.rearrange("(o one) -> o one", one=1))
+        small_rows = keep.tile([P, P], BF16, name="small_rows")
+        nc.vector.memset(small_rows[:], 0.0)
+        nc.vector.memset(small_rows[ONES_ROW : ONES_ROW + 1, :], 1.0)
+        small_picks = keep.tile([P, SPREAD_COLS], BF16, name="small_picks")
+        nc.vector.memset(small_picks[:], 0.0)
+        nc.vector.memset(small_picks[0:1, 0:1], 1.0)
+        nc.scalar.dma_start(out=small_rows[0:1, :], in_=b_fuse.rearrange("(one o) -> one o", one=1))
+        nc.scalar.dma_start(
+            out=small_picks[ONES_ROW : ONES_ROW + 1, 1:2], in_=gamma.rearrange("(one g) -> one g", one=1)
+        )
+
 
         att_rows = attention.rearrange("b (m t) d -> b m t d", t=PACK)
         v_rows = v.rearrange("b (p j) n -> b p j n", j=PACK)
@@ -108,10 +118,6 @@ def tile_gcam_pb_s_kernel(tc, attention, v, x, wf, b_fuse, gamma, out):
 
         ident = keep.tile([P, P], F32, name="ident")
         masks.make_identity(nc, ident[:])
-        gamma_f32 = keep.tile([P, 1], F32, name="gamma_f32")
-        nc.gpsimd.tensor_copy(out=gamma_f32[:], in_=gamma_bf[:])
-        bias_f32 = keep.tile([P, 1], F32, name="bias_f32")
-        nc.gpsimd.tensor_copy(out=bias_f32[:], in_=bias_bf[:])
         table_warm = keep.tile([P, 1], F32, name="table_warm")
         nc.scalar.activation(out=table_warm[:], in_=ident[:, 0:1], func=ACT.Identity)
 
@@ -159,7 +165,7 @@ def tile_gcam_pb_s_kernel(tc, attention, v, x, wf, b_fuse, gamma, out):
                 nc.vector.scalar_tensor_tensor(
                     out=z_grouped[b][:, cols].rearrange("m (n t) -> m n t", t=PACK),
                     in0=mixed[b, h][:].rearrange("m t n -> m n t"),
-                    scalar=gamma_f32[:, 0:1],
+                    scalar=small[:, 1:2],
                     in1=v_grouped[b][:, cols].rearrange("m (n t) -> m n t", t=PACK),
                     op0=ALU.mult,
                     op1=ALU.add,
@@ -173,12 +179,16 @@ def tile_gcam_pb_s_kernel(tc, attention, v, x, wf, b_fuse, gamma, out):
 
         def add_bias_and_store(b):
             result = keep.tile([P, POSITIONS], F32, name="result_%d" % b)
-            nc.scalar.activation(out=result[:], in_=fused[b][:], func=ACT.Identity, bias=bias_f32[:, 0:1])
+            nc.scalar.activation(out=result[:], in_=fused[b][:], func=ACT.Identity, bias=small[:, 0:1])
             nc.sync.dma_start(out=out[b], in_=result[:])
 
         flip_attention(0)
         quantise_stage_1(0)
         flip_attention(1)
+        spread = small_bank.tile([P, SPREAD_COLS], F32, name="spread")
+        nc.tensor.matmul(out=spread[:], lhsT=small_rows[:], rhs=small_picks[:], start=True, stop=True)
+        small = keep.tile([P, 2], F32, name="small")
+        nc.scalar.copy(out=small[:], in_=spread[:, 0:2])
         mix(0)
         quantise_stage_1(1)
         wf_flipped = flip_k_last(nc, banks, ident, wf_sb)

@@ -28,7 +28,7 @@ FLOPS = 2 * IMAGES * POSITIONS * (CHANNELS * CHANNELS + OUT_CHANNELS * 2 * CHANN
 
 
 def flip_k_last(nc, banks, ident, rows):
-    words = rows[:].bitcast(F32).rearrange("r (s p u) -> r s u p", s=2, u=PAIR)
+    words = rows[:].bitcast(F32).rearrange("r (s u p) -> r s u p", s=2, u=PAIR)
     flipped = banks.tile([P, 2, PAIR, P], F32, name="flipped")
     for s in range(2):
         for u in range(PAIR):
@@ -95,26 +95,23 @@ def tile_gcam_pb_s_kernel(tc, attention, v, x, wf, b_fuse, gamma, out):
         )
 
 
-        att_rows = attention.rearrange("b (m t) d -> b m t d", t=PACK)
-        v_rows = v.rearrange("b (p j) n -> b p j n", j=PACK)
-        x_rows = x.rearrange("b (p j) n -> b p j n", j=PACK)
+        att_rows = attention.rearrange("b (u m e) d -> b u m (e d)", u=2, e=PAIR)
+        v_rows = v.rearrange("b (u p e) n -> b p u (e n)", u=2, e=PAIR)
+        x_rows = x.rearrange("b (u p e) n -> b p u (e n)", u=2, e=PAIR)
         att_sb = {}
         v_sb = {}
         x_sb = {}
         for b in range(IMAGES):
             for s in range(2):
                 att_sb[b, s] = keep.tile([P, 2 * CHANNELS], BF16, name="att_sb_%d%d" % (b, s))
-                nc.sync.dma_start(
-                    out=att_sb[b, s][:].rearrange("m (t d) -> m t d", t=2),
-                    in_=att_rows[b, :, 2 * s : 2 * s + 2, :],
-                )
+                nc.sync.dma_start(out=att_sb[b, s][:], in_=att_rows[b, s])
             v_sb[b] = keep.tile([P, PACK, POSITIONS], BF16, name="v_sb_%d" % b)
-            nc.sync.dma_start(out=v_sb[b][:], in_=v_rows[b])
+            nc.sync.dma_start(out=v_sb[b][:].rearrange("p (u e) n -> p u (e n)", u=2), in_=v_rows[b])
         wf_sb = keep.tile([P, 2 * CHANNELS], BF16, name="wf_sb")
         nc.sync.dma_start(out=wf_sb[:], in_=wf)
         for b in range(IMAGES):
             x_sb[b] = keep.tile([P, PACK, POSITIONS], BF16, name="x_sb_%d" % b)
-            nc.sync.dma_start(out=x_sb[b][:], in_=x_rows[b])
+            nc.sync.dma_start(out=x_sb[b][:].rearrange("p (u e) n -> p u (e n)", u=2), in_=x_rows[b])
 
         ident = keep.tile([P, P], F32, name="ident")
         masks.make_identity(nc, ident[:])

@@ -78,8 +78,8 @@ def tile_gcam_pb_s_kernel(tc, attention, v, x, wf, b_fuse, gamma, out):
     with ExitStack() as ctx:
         keep = ctx.enter_context(tc.tile_pool(name="keep", bufs=1))
         banks = ctx.enter_context(tc.psum_pool(name="banks", bufs=2))
-        mixed_banks = ctx.enter_context(tc.psum_pool(name="mixed_banks", bufs=3))
-        fused_banks = ctx.enter_context(tc.psum_pool(name="fused_banks", bufs=2))
+        mixed_banks = ctx.enter_context(tc.psum_pool(name="mixed_banks", bufs=2))
+        fused_banks = ctx.enter_context(tc.psum_pool(name="fused_banks", bufs=3))
         small_bank = ctx.enter_context(tc.psum_pool(name="small_bank", bufs=1))
         ctx.enter_context(tc.manual_schedule())
 
@@ -101,17 +101,29 @@ def tile_gcam_pb_s_kernel(tc, attention, v, x, wf, b_fuse, gamma, out):
         att_sb = {}
         v_sb = {}
         x_sb = {}
-        for b in range(IMAGES):
-            for s in range(2):
-                att_sb[b, s] = keep.tile([P, 2 * CHANNELS], BF16, name="att_sb_%d%d" % (b, s))
-                nc.sync.dma_start(out=att_sb[b, s][:], in_=att_rows[b, s])
+        wf_sb = keep.tile([P, 2 * CHANNELS], BF16, name="wf_sb")
+
+        def load_attention(b, s):
+            att_sb[b, s] = keep.tile([P, 2 * CHANNELS], BF16, name="att_sb_%d%d" % (b, s))
+            nc.sync.dma_start(out=att_sb[b, s][:], in_=att_rows[b, s])
+
+        def load_v(b):
             v_sb[b] = keep.tile([P, PACK, POSITIONS], BF16, name="v_sb_%d" % b)
             nc.sync.dma_start(out=v_sb[b][:].rearrange("p (u e) n -> p u (e n)", u=2), in_=v_rows[b])
-        wf_sb = keep.tile([P, 2 * CHANNELS], BF16, name="wf_sb")
-        nc.sync.dma_start(out=wf_sb[:], in_=wf)
-        for b in range(IMAGES):
+
+        def load_x(b):
             x_sb[b] = keep.tile([P, PACK, POSITIONS], BF16, name="x_sb_%d" % b)
             nc.sync.dma_start(out=x_sb[b][:].rearrange("p (u e) n -> p u (e n)", u=2), in_=x_rows[b])
+
+        load_attention(0, 0)
+        load_attention(0, 1)
+        load_v(0)
+        load_attention(1, 0)
+        load_attention(1, 1)
+        load_v(1)
+        nc.sync.dma_start(out=wf_sb[:], in_=wf)
+        load_x(0)
+        load_x(1)
 
         ident = keep.tile([P, P], F32, name="ident")
         masks.make_identity(nc, ident[:])
@@ -128,17 +140,29 @@ def tile_gcam_pb_s_kernel(tc, attention, v, x, wf, b_fuse, gamma, out):
         x_grouped = {}
         x_mx = {}
         fused = {}
+        wf_flipped = []
+        wf_grouped = []
+        wf_mx = []
+        small = keep.tile([P, 2], F32, name="small")
 
-        def flip_attention(b):
-            for s in range(2):
-                flipped = flip_k_last(nc, banks, ident, att_sb[b, s])
-                att_grouped[b, s] = leave_psum(nc, keep, flipped, "att_%d%d" % (b, s))
+        def flip_attention(b, s):
+            flipped = flip_k_last(nc, banks, ident, att_sb[b, s])
+            att_grouped[b, s] = leave_psum(nc, keep, flipped, "att_%d%d" % (b, s))
 
-        def quantise_stage_1(b):
+        def group_v(b):
             v_grouped[b] = regroup_k_first(nc.vector.tensor_copy, keep, v_sb[b], "v_%d" % b)
-            att_mx[b, 0] = quantise(nc, keep, att_grouped[b, 0], "att_%d0" % b)
+
+        def group_x(b):
+            x_grouped[b] = regroup_k_first(nc.scalar.copy, keep, x_sb[b], "x_%d" % b)
+
+        def quantise_attention(b, s):
+            att_mx[b, s] = quantise(nc, keep, att_grouped[b, s], "att_%d%d" % (b, s))
+
+        def quantise_v(b):
             v_mx[b] = quantise(nc, keep, v_grouped[b], "v_%d" % b)
-            att_mx[b, 1] = quantise(nc, keep, att_grouped[b, 1], "att_%d1" % b)
+
+        def quantise_x(b):
+            x_mx[b] = quantise(nc, keep, x_grouped[b], "x_%d" % b)
 
         def mix(b):
             for h in range(HALVES):
@@ -155,52 +179,107 @@ def tile_gcam_pb_s_kernel(tc, attention, v, x, wf, b_fuse, gamma, out):
                         True,
                     )
 
-        def add_v(b):
-            z_grouped[b] = keep.tile([P, POSITIONS * PACK], BF16, align_bytes=64, name="z_grouped_%d" % b)
-            for h in range(HALVES):
-                cols = slice(h * P * PACK, (h + 1) * P * PACK)
-                nc.vector.scalar_tensor_tensor(
-                    out=z_grouped[b][:, cols].rearrange("m (n t) -> m n t", t=PACK),
-                    in0=mixed[b, h][:].rearrange("m t n -> m n t"),
-                    scalar=small[:, 1:2],
-                    in1=v_grouped[b][:, cols].rearrange("m (n t) -> m n t", t=PACK),
-                    op0=ALU.mult,
-                    op1=ALU.add,
-                )
+        def add_v(b, h):
+            if h == 0:
+                z_grouped[b] = keep.tile([P, POSITIONS * PACK], BF16, align_bytes=64, name="z_grouped_%d" % b)
+            cols = slice(h * P * PACK, (h + 1) * P * PACK)
+            nc.vector.scalar_tensor_tensor(
+                out=z_grouped[b][:, cols].rearrange("m (n t) -> m n t", t=PACK),
+                in0=mixed[b, h][:].rearrange("m t n -> m n t"),
+                scalar=small[:, 1:2],
+                in1=v_grouped[b][:, cols].rearrange("m (n t) -> m n t", t=PACK),
+                op0=ALU.mult,
+                op1=ALU.add,
+            )
+
+        def quantise_z(b):
+            z_mx[b] = quantise(nc, keep, z_grouped[b], "z_%d" % b)
+
+        def quantise_z_half(b, h):
+            if h == 0:
+                codes = keep.tile([P, POSITIONS], U32, align_bytes=64, name="codes_z_%d" % b)
+                scales = keep.tile([P, POSITIONS], U8, align_bytes=64, name="scales_z_%d" % b)
+                z_mx[b] = (codes, scales)
+            cols = slice(h * P, (h + 1) * P)
+            nc.vector.quantize_mx(
+                out=z_mx[b][0][:, cols].bitcast(FP8X4),
+                scales=z_mx[b][1][:, cols],
+                in_=z_grouped[b][:, h * P * PACK : (h + 1) * P * PACK],
+            )
 
         def fuse(b):
             every = slice(0, POSITIONS)
             fused[b] = fused_banks.tile([P, POSITIONS], F32, name="fused")
-            multiply(nc, fused[b][:], wf_mx, slice(P, 2 * P), x_mx[b], every, True, False)
-            multiply(nc, fused[b][:], wf_mx, slice(0, P), z_mx[b], every, False, True)
+            multiply(nc, fused[b][:], wf_mx[0], slice(P, 2 * P), x_mx[b], every, True, False)
+            multiply(nc, fused[b][:], wf_mx[0], slice(0, P), z_mx[b], every, False, True)
+
+        def fuse_x_half(b, h):
+            cols = slice(h * P, (h + 1) * P)
+            fused[b, h] = fused_banks.tile([P, P], F32, name="fused")
+            multiply(nc, fused[b, h][:], wf_mx[0], slice(P, 2 * P), x_mx[b], cols, True, False)
+
+        def fuse_z_half(b, h):
+            cols = slice(h * P, (h + 1) * P)
+            multiply(nc, fused[b, h][:], wf_mx[0], slice(0, P), z_mx[b], cols, False, True)
 
         def add_bias_and_store(b):
             result = keep.tile([P, POSITIONS], F32, name="result_%d" % b)
             nc.scalar.activation(out=result[:], in_=fused[b][:], func=ACT.Identity, bias=small[:, 0:1])
             nc.sync.dma_start(out=out[b], in_=result[:])
 
-        flip_attention(0)
-        quantise_stage_1(0)
-        flip_attention(1)
-        spread = small_bank.tile([P, SPREAD_COLS], F32, name="spread")
-        nc.tensor.matmul(out=spread[:], lhsT=small_rows[:], rhs=small_picks[:], start=True, stop=True)
-        small = keep.tile([P, 2], F32, name="small")
-        nc.scalar.copy(out=small[:], in_=spread[:, 0:2])
+        def add_bias_and_store_half(b, h):
+            result = keep.tile([P, P], F32, name="result_%d%d" % (b, h))
+            nc.scalar.activation(out=result[:], in_=fused[b, h][:], func=ACT.Identity, bias=small[:, 0:1])
+            nc.sync.dma_start(out=out[b, :, h * P : (h + 1) * P], in_=result[:])
+
+        def spread_small():
+            spread = small_bank.tile([P, SPREAD_COLS], F32, name="spread")
+            nc.tensor.matmul(out=spread[:], lhsT=small_rows[:], rhs=small_picks[:], start=True, stop=True)
+            nc.scalar.copy(out=small[:], in_=spread[:, 0:2])
+
+        def flip_wf():
+            wf_flipped.append(flip_k_last(nc, banks, ident, wf_sb))
+
+        def leave_wf():
+            wf_grouped.append(leave_psum(nc, keep, wf_flipped[0], "wf"))
+
+        def quantise_wf():
+            wf_mx.append(quantise(nc, keep, wf_grouped[0], "wf"))
+
+        flip_attention(0, 0)
+        flip_attention(0, 1)
+        group_v(0)
+        quantise_attention(0, 0)
+        quantise_v(0)
+        quantise_attention(0, 1)
+        flip_attention(1, 0)
+        flip_attention(1, 1)
+        spread_small()
         mix(0)
-        quantise_stage_1(1)
-        wf_flipped = flip_k_last(nc, banks, ident, wf_sb)
+        group_v(1)
+        quantise_attention(1, 0)
+        quantise_v(1)
+        quantise_attention(1, 1)
+        flip_wf()
         mix(1)
-        x_grouped[0] = regroup_k_first(nc.scalar.copy, keep, x_sb[0], "x_0")
-        wf_grouped = leave_psum(nc, keep, wf_flipped, "wf")
-        x_grouped[1] = regroup_k_first(nc.scalar.copy, keep, x_sb[1], "x_1")
-        add_v(0)
-        x_mx[0] = quantise(nc, keep, x_grouped[0], "x_0")
-        z_mx[0] = quantise(nc, keep, z_grouped[0], "z_0")
-        wf_mx = quantise(nc, keep, wf_grouped, "wf")
+        group_x(0)
+        leave_wf()
+        group_x(1)
+        add_v(0, 0)
+        add_v(0, 1)
+        quantise_x(0)
+        quantise_z(0)
+        quantise_wf()
         fuse(0)
-        add_v(1)
-        x_mx[1] = quantise(nc, keep, x_grouped[1], "x_1")
-        z_mx[1] = quantise(nc, keep, z_grouped[1], "z_1")
+        add_v(1, 0)
+        add_v(1, 1)
+        quantise_x(1)
+        fuse_x_half(1, 0)
+        fuse_x_half(1, 1)
+        quantise_z_half(1, 0)
+        quantise_z_half(1, 1)
         add_bias_and_store(0)
-        fuse(1)
-        add_bias_and_store(1)
+        fuse_z_half(1, 0)
+        add_bias_and_store_half(1, 0)
+        fuse_z_half(1, 1)
+        add_bias_and_store_half(1, 1)

@@ -83,16 +83,23 @@ def tile_gcam_pb_s_kernel(tc, attention, v, x, wf, b_fuse, gamma, out):
         small_bank = ctx.enter_context(tc.psum_pool(name="small_bank", bufs=1))
         ctx.enter_context(tc.manual_schedule())
 
+        zero_column = keep.tile([P, 1], F32, name="zero_column")
+        nc.vector.memset(zero_column[:], 0.0)
+        table_warm = keep.tile([P, 1], F32, name="table_warm")
+        nc.scalar.activation(out=table_warm[:], in_=zero_column[:], func=ACT.Identity)
+
         small_rows = keep.tile([P, P], BF16, name="small_rows")
         nc.vector.memset(small_rows[:], 0.0)
         nc.vector.memset(small_rows[ONES_ROW : ONES_ROW + 1, :], 1.0)
         small_picks = keep.tile([P, SPREAD_COLS], BF16, name="small_picks")
         nc.vector.memset(small_picks[:], 0.0)
         nc.vector.memset(small_picks[0:1, 0:1], 1.0)
-        nc.scalar.dma_start(out=small_rows[0:1, :], in_=b_fuse.rearrange("(one o) -> one o", one=1))
-        nc.scalar.dma_start(
-            out=small_picks[ONES_ROW : ONES_ROW + 1, 1:2], in_=gamma.rearrange("(one g) -> one g", one=1)
-        )
+
+        def load_small():
+            nc.sync.dma_start(out=small_rows[0:1, :], in_=b_fuse.rearrange("(one o) -> one o", one=1))
+            nc.sync.dma_start(
+                out=small_picks[ONES_ROW : ONES_ROW + 1, 1:2], in_=gamma.rearrange("(one g) -> one g", one=1)
+            )
 
 
         att_rows = attention.rearrange("b (u m e) d -> b u m (e d)", u=2, e=PAIR)
@@ -120,6 +127,7 @@ def tile_gcam_pb_s_kernel(tc, attention, v, x, wf, b_fuse, gamma, out):
         load_v(0)
         load_attention(1, 0)
         load_attention(1, 1)
+        load_small()
         load_v(1)
         nc.sync.dma_start(out=wf_sb[:], in_=wf)
         load_x(0)
@@ -127,8 +135,6 @@ def tile_gcam_pb_s_kernel(tc, attention, v, x, wf, b_fuse, gamma, out):
 
         ident = keep.tile([P, P], F32, name="ident")
         masks.make_identity(nc, ident[:])
-        table_warm = keep.tile([P, 1], F32, name="table_warm")
-        nc.scalar.activation(out=table_warm[:], in_=ident[:, 0:1], func=ACT.Identity)
 
         att_grouped = {}
         att_mx = {}
@@ -151,6 +157,15 @@ def tile_gcam_pb_s_kernel(tc, attention, v, x, wf, b_fuse, gamma, out):
 
         def group_v(b):
             v_grouped[b] = regroup_k_first(nc.vector.tensor_copy, keep, v_sb[b], "v_%d" % b)
+
+        def group_v_on_scalar(b):
+            v_grouped[b] = regroup_k_first(nc.scalar.copy, keep, v_sb[b], "v_%d" % b)
+
+        def copy_on_gpsimd(out, in_):
+            nc.gpsimd.tensor_scalar(out=out, in0=in_, scalar1=1.0, scalar2=0.0, op0=ALU.mult, op1=ALU.add)
+
+        def group_x_on_gpsimd(b):
+            x_grouped[b] = regroup_k_first(copy_on_gpsimd, keep, x_sb[b], "x_%d" % b)
 
         def group_x(b):
             x_grouped[b] = regroup_k_first(nc.scalar.copy, keep, x_sb[b], "x_%d" % b)

@@ -22,6 +22,7 @@ POSITIONS = 256
 OUT_CHANNELS = 128
 HALVES = POSITIONS // P
 ONES_ROW = 32
+GAMMA_COL = 2
 SPREAD_COLS = 32
 
 FLOPS = 2 * IMAGES * POSITIONS * (CHANNELS * CHANNELS + OUT_CHANNELS * 2 * CHANNELS)
@@ -98,7 +99,7 @@ def tile_gcam_pb_s_kernel(tc, attention, v, x, wf, b_fuse, gamma, out):
         def load_small():
             nc.sync.dma_start(out=small_rows[0:1, :], in_=b_fuse.rearrange("(one o) -> one o", one=1))
             nc.sync.dma_start(
-                out=small_picks[ONES_ROW : ONES_ROW + 1, 1:2], in_=gamma.rearrange("(one g) -> one g", one=1)
+                out=small_picks[ONES_ROW : ONES_ROW + 1, GAMMA_COL : GAMMA_COL + 1], in_=gamma.rearrange("(one g) -> one g", one=1)
             )
 
 
@@ -149,7 +150,7 @@ def tile_gcam_pb_s_kernel(tc, attention, v, x, wf, b_fuse, gamma, out):
         wf_flipped = []
         wf_grouped = []
         wf_mx = []
-        small = keep.tile([P, 2], F32, name="small")
+        small = keep.tile([P, GAMMA_COL + 1], F32, name="small")
 
         def flip_attention(b, s):
             flipped = flip_k_last(nc, banks, ident, att_sb[b, s])
@@ -166,6 +167,9 @@ def tile_gcam_pb_s_kernel(tc, attention, v, x, wf, b_fuse, gamma, out):
 
         def group_x_on_gpsimd(b):
             x_grouped[b] = regroup_k_first(copy_on_gpsimd, keep, x_sb[b], "x_%d" % b)
+
+        def group_x_on_vector(b):
+            x_grouped[b] = regroup_k_first(nc.vector.tensor_copy, keep, x_sb[b], "x_%d" % b)
 
         def group_x(b):
             x_grouped[b] = regroup_k_first(nc.scalar.copy, keep, x_sb[b], "x_%d" % b)
@@ -201,7 +205,7 @@ def tile_gcam_pb_s_kernel(tc, attention, v, x, wf, b_fuse, gamma, out):
             nc.vector.scalar_tensor_tensor(
                 out=z_grouped[b][:, cols].rearrange("m (n t) -> m n t", t=PACK),
                 in0=mixed[b, h][:].rearrange("m t n -> m n t"),
-                scalar=small[:, 1:2],
+                scalar=small[:, GAMMA_COL : GAMMA_COL + 1],
                 in1=v_grouped[b][:, cols].rearrange("m (n t) -> m n t", t=PACK),
                 op0=ALU.mult,
                 op1=ALU.add,
@@ -247,10 +251,15 @@ def tile_gcam_pb_s_kernel(tc, attention, v, x, wf, b_fuse, gamma, out):
             nc.scalar.activation(out=result[:], in_=fused[b, h][:], func=ACT.Identity, bias=small[:, 0:1])
             nc.sync.dma_start(out=out[b, :, h * P : (h + 1) * P], in_=result[:])
 
+        def add_bias_on_vector_and_store_half(b, h):
+            result = keep.tile([P, P], F32, name="result_%d%d" % (b, h))
+            nc.vector.tensor_scalar_add(out=result[:], in0=fused[b, h][:], scalar1=small[:, 0:1])
+            nc.sync.dma_start(out=out[b, :, h * P : (h + 1) * P], in_=result[:])
+
         def spread_small():
             spread = small_bank.tile([P, SPREAD_COLS], F32, name="spread")
             nc.tensor.matmul(out=spread[:], lhsT=small_rows[:], rhs=small_picks[:], start=True, stop=True)
-            nc.scalar.copy(out=small[:], in_=spread[:, 0:2])
+            nc.scalar.copy(out=small[:], in_=spread[:, 0 : GAMMA_COL + 1])
 
         def flip_wf():
             wf_flipped.append(flip_k_last(nc, banks, ident, wf_sb))

@@ -14,6 +14,7 @@ ACT = mybir.ActivationFunctionType
 P = 128
 PACK = 4
 K_PASS = P * PACK
+RUN = 8
 PAIR = 2
 
 IMAGES = 2
@@ -49,8 +50,8 @@ def leave_psum(nc, keep, flipped, label):
 def regroup_k_first(copy, keep, rows, label):
     grouped = keep.tile([P, POSITIONS * PACK], BF16, align_bytes=64, name="grouped_" + label)
     copy(
-        out=grouped[:].rearrange("p (c i j) -> p c j i", i=4, j=PACK),
-        in_=rows[:].rearrange("p j (c i) -> p c j i", i=4),
+        out=grouped[:].rearrange("p (c i j) -> p c j i", i=RUN, j=PACK),
+        in_=rows[:].rearrange("p j (c i) -> p c j i", i=RUN),
     )
     return grouped
 

@@ -24,6 +24,7 @@ OUT_CHANNELS = 128
 HALVES = POSITIONS // P
 ONES_ROW = 32
 GAMMA_COL = 2
+WARM_COLS = 512
 SPREAD_COLS = 32
 
 FLOPS = 2 * IMAGES * POSITIONS * (CHANNELS * CHANNELS + OUT_CHANNELS * 2 * CHANNELS)
@@ -89,6 +90,11 @@ def tile_gcam_pb_s_kernel(tc, attention, v, x, wf, b_fuse, gamma, out):
         nc.vector.memset(zero_column[:], 0.0)
         table_warm = keep.tile([P, 1], F32, name="table_warm")
         nc.scalar.activation(out=table_warm[:], in_=zero_column[:], func=ACT.Identity)
+
+        zeros = keep.tile([P, WARM_COLS], F32, name="zeros")
+        nc.gpsimd.memset(zeros[:], 0.0)
+        unread = small_bank.tile([P, WARM_COLS], F32, name="spread")
+        nc.tensor.matmul(out=unread[:], lhsT=zeros[:, 0:P], rhs=zeros[:], start=True, stop=True)
 
         small_rows = keep.tile([P, P], BF16, name="small_rows")
         nc.vector.memset(small_rows[:], 0.0)
@@ -171,6 +177,17 @@ def tile_gcam_pb_s_kernel(tc, attention, v, x, wf, b_fuse, gamma, out):
 
         def group_x_on_vector(b):
             x_grouped[b] = regroup_k_first(nc.vector.tensor_copy, keep, x_sb[b], "x_%d" % b)
+
+        def regroup_half(copy, grouped, rows, h):
+            copy(
+                out=grouped[:, h * P * PACK : (h + 1) * P * PACK].rearrange("p (c i j) -> p c j i", i=RUN, j=PACK),
+                in_=rows[:, :, h * P : (h + 1) * P].rearrange("p j (c i) -> p c j i", i=RUN),
+            )
+
+        def group_x_half(b, h, copy):
+            if h == 0:
+                x_grouped[b] = keep.tile([P, POSITIONS * PACK], BF16, align_bytes=64, name="grouped_x_%d" % b)
+            regroup_half(copy, x_grouped[b], x_sb[b], h)
 
         def group_x(b):
             x_grouped[b] = regroup_k_first(nc.scalar.copy, keep, x_sb[b], "x_%d" % b)

from contextlib import ExitStack

import concourse.masks as masks
import concourse.mybir as mybir

BF16 = mybir.dt.bfloat16
F32 = mybir.dt.float32
U32 = mybir.dt.uint32
U8 = mybir.dt.uint8
FP8X4 = mybir.dt.float8_e4m3fn_x4
ALU = mybir.AluOpType
ACT = mybir.ActivationFunctionType

P = 128
PACK = 4
K_PASS = P * PACK
RUN = 8
PAIR = 2

IMAGES = 2
CHANNELS = 512
POSITIONS = 256
OUT_CHANNELS = 128
HALVES = POSITIONS // P
ONES_ROW = 32
GAMMA_COL = 2
WARM_COLS = 512
SPREAD_COLS = 32

FLOPS = 2 * IMAGES * POSITIONS * (CHANNELS * CHANNELS + OUT_CHANNELS * 2 * CHANNELS)


def flip_k_last(nc, banks, ident, rows):
    words = rows[:].bitcast(F32).rearrange("r (s u p) -> r s u p", s=2, u=PAIR)
    flipped = banks.tile([P, 2, PAIR, P], F32, name="flipped")
    for s in range(2):
        for u in range(PAIR):
            nc.tensor.transpose(flipped[:, s, u, :], words[:, s, u, :], ident[:])
    return flipped


def leave_psum(nc, keep, flipped, label):
    grouped = keep.tile([P, 2 * P * PACK], BF16, align_bytes=64, name="grouped_" + label)
    nc.scalar.copy(
        out=grouped[:].bitcast(F32).rearrange("p (s r u) -> p s r u", s=2, u=PAIR),
        in_=flipped[:].rearrange("p s u r -> p s r u"),
    )
    return grouped


def regroup_k_first(copy, keep, rows, label):
    grouped = keep.tile([P, POSITIONS * PACK], BF16, align_bytes=64, name="grouped_" + label)
    copy(
        out=grouped[:].rearrange("p (c i j) -> p c j i", i=RUN, j=PACK),
        in_=rows[:].rearrange("p j (c i) -> p c j i", i=RUN),
    )
    return grouped


def quantise(nc, keep, grouped, label):
    codes = keep.tile([P, POSITIONS], U32, align_bytes=64, name="codes_" + label)
    scales = keep.tile([P, POSITIONS], U8, align_bytes=64, name="scales_" + label)
    nc.vector.quantize_mx(out=codes[:].bitcast(FP8X4), scales=scales[:], in_=grouped[:])
    return codes, scales


def multiply(nc, acc, weights, w_cols, moving, n_cols, start, stop):
    nc.tensor.matmul_mx(
        out=acc,
        lhsT=weights[0][:, w_cols].bitcast(FP8X4),
        lhsT_scale=weights[1][:, w_cols],
        rhs=moving[0][:, n_cols].bitcast(FP8X4),
        rhs_scale=moving[1][:, n_cols],
        start=start,
        stop=stop,
    )


def tile_gcam_pb_s_kernel(tc, attention, v, x, wf, b_fuse, gamma, out):
    nc = tc.nc
    with ExitStack() as ctx:
        keep = ctx.enter_context(tc.tile_pool(name="keep", bufs=1))
        banks = ctx.enter_context(tc.psum_pool(name="banks", bufs=2))
        mixed_banks = ctx.enter_context(tc.psum_pool(name="mixed_banks", bufs=2))
        fused_banks = ctx.enter_context(tc.psum_pool(name="fused_banks", bufs=3))
        small_bank = ctx.enter_context(tc.psum_pool(name="small_bank", bufs=1))
        ctx.enter_context(tc.manual_schedule())

        zero_column = keep.tile([P, 1], F32, name="zero_column")
        nc.vector.memset(zero_column[:], 0.0)
        table_warm = keep.tile([P, 1], F32, name="table_warm")
        nc.scalar.activation(out=table_warm[:], in_=zero_column[:], func=ACT.Identity)

        zeros = keep.tile([P, WARM_COLS], F32, name="zeros")
        nc.gpsimd.memset(zeros[:], 0.0)
        unread = small_bank.tile([P, WARM_COLS], F32, name="spread")
        nc.tensor.matmul(out=unread[:], lhsT=zeros[:, 0:P], rhs=zeros[:], start=True, stop=True)

        small_rows = keep.tile([P, P], BF16, name="small_rows")
        nc.vector.memset(small_rows[:], 0.0)
        nc.vector.memset(small_rows[ONES_ROW : ONES_ROW + 1, :], 1.0)
        small_picks = keep.tile([P, SPREAD_COLS], BF16, name="small_picks")
        nc.vector.memset(small_picks[:], 0.0)
        nc.vector.memset(small_picks[0:1, 0:1], 1.0)

        def load_small():
            nc.sync.dma_start(out=small_rows[0:1, :], in_=b_fuse.rearrange("(one o) -> one o", one=1))
            nc.sync.dma_start(
                out=small_picks[ONES_ROW : ONES_ROW + 1, GAMMA_COL : GAMMA_COL + 1], in_=gamma.rearrange("(one g) -> one g", one=1)
            )


        att_rows = attention.rearrange("b (u m e) d -> b u m (e d)", u=2, e=PAIR)
        v_rows = v.rearrange("b (u p e) n -> b p u (e n)", u=2, e=PAIR)
        x_rows = x.rearrange("b (u p e) n -> b p u (e n)", u=2, e=PAIR)
        att_sb = {}
        v_sb = {}
        x_sb = {}
        wf_sb = keep.tile([P, 2 * CHANNELS], BF16, name="wf_sb")

        def load_attention(b, s):
            att_sb[b, s] = keep.tile([P, 2 * CHANNELS], BF16, name="att_sb_%d%d" % (b, s))
            nc.sync.dma_start(out=att_sb[b, s][:], in_=att_rows[b, s])

        def load_v(b):
            v_sb[b] = keep.tile([P, PACK, POSITIONS], BF16, name="v_sb_%d" % b)
            nc.sync.dma_start(out=v_sb[b][:].rearrange("p (u e) n -> p u (e n)", u=2), in_=v_rows[b])

        def load_x(b):
            x_sb[b] = keep.tile([P, PACK, POSITIONS], BF16, name="x_sb_%d" % b)
            nc.sync.dma_start(out=x_sb[b][:].rearrange("p (u e) n -> p u (e n)", u=2), in_=x_rows[b])

        load_attention(0, 0)
        load_attention(0, 1)
        load_v(0)
        load_attention(1, 0)
        load_attention(1, 1)
        load_small()
        load_v(1)
        nc.sync.dma_start(out=wf_sb[:], in_=wf)
        load_x(0)
        load_x(1)

        ident = keep.tile([P, P], F32, name="ident")
        masks.make_identity(nc, ident[:])

        att_grouped = {}
        att_mx = {}
        v_grouped = {}
        v_mx = {}
        mixed = {}
        z_grouped = {}
        z_mx = {}
        x_grouped = {}
        x_mx = {}
        fused = {}
        wf_flipped = []
        wf_grouped = []
        wf_mx = []
        small = keep.tile([P, GAMMA_COL + 1], F32, name="small")

        def flip_attention(b, s):
            flipped = flip_k_last(nc, banks, ident, att_sb[b, s])
            att_grouped[b, s] = leave_psum(nc, keep, flipped, "att_%d%d" % (b, s))

        def group_v(b):
            v_grouped[b] = regroup_k_first(nc.vector.tensor_copy, keep, v_sb[b], "v_%d" % b)

        def group_v_on_scalar(b):
            v_grouped[b] = regroup_k_first(nc.scalar.copy, keep, v_sb[b], "v_%d" % b)

        def copy_on_gpsimd(out, in_):
            nc.gpsimd.tensor_scalar(out=out, in0=in_, scalar1=1.0, scalar2=0.0, op0=ALU.mult, op1=ALU.add)

        def group_x_on_gpsimd(b):
            x_grouped[b] = regroup_k_first(copy_on_gpsimd, keep, x_sb[b], "x_%d" % b)

        def group_x_on_vector(b):
            x_grouped[b] = regroup_k_first(nc.vector.tensor_copy, keep, x_sb[b], "x_%d" % b)

        def regroup_half(copy, grouped, rows, h):
            copy(
                out=grouped[:, h * P * PACK : (h + 1) * P * PACK].rearrange("p (c i j) -> p c j i", i=RUN, j=PACK),
                in_=rows[:, :, h * P : (h + 1) * P].rearrange("p j (c i) -> p c j i", i=RUN),
            )

        def group_x_half(b, h, copy):
            if h == 0:
                x_grouped[b] = keep.tile([P, POSITIONS * PACK], BF16, align_bytes=64, name="grouped_x_%d" % b)
            regroup_half(copy, x_grouped[b], x_sb[b], h)

        def group_x(b):
            x_grouped[b] = regroup_k_first(nc.scalar.copy, keep, x_sb[b], "x_%d" % b)

        def quantise_attention(b, s):
            att_mx[b, s] = quantise(nc, keep, att_grouped[b, s], "att_%d%d" % (b, s))

        def quantise_v(b):
            v_mx[b] = quantise(nc, keep, v_grouped[b], "v_%d" % b)

        def quantise_x(b):
            x_mx[b] = quantise(nc, keep, x_grouped[b], "x_%d" % b)

        def mix(b):
            for h in range(HALVES):
                mixed[b, h] = mixed_banks.tile([P, PACK, P], F32, name="mixed")
                for t in range(PACK):
                    multiply(
                        nc,
                        mixed[b, h][:, t, :],
                        att_mx[b, t // 2],
                        slice((t % 2) * P, (t % 2 + 1) * P),
                        v_mx[b],
                        slice(h * P, (h + 1) * P),
                        True,
                        True,
                    )

        def add_v(b, h):
            if h == 0:
                z_grouped[b] = keep.tile([P, POSITIONS * PACK], BF16, align_bytes=64, name="z_grouped_%d" % b)
            cols = slice(h * P * PACK, (h + 1) * P * PACK)
            nc.vector.scalar_tensor_tensor(
                out=z_grouped[b][:, cols].rearrange("m (n t) -> m n t", t=PACK),
                in0=mixed[b, h][:].rearrange("m t n -> m n t"),
                scalar=small[:, GAMMA_COL : GAMMA_COL + 1],
                in1=v_grouped[b][:, cols].rearrange("m (n t) -> m n t", t=PACK),
                op0=ALU.mult,
                op1=ALU.add,
            )

        def quantise_z(b):
            z_mx[b] = quantise(nc, keep, z_grouped[b], "z_%d" % b)

        def quantise_z_half(b, h):
            if h == 0:
                codes = keep.tile([P, POSITIONS], U32, align_bytes=64, name="codes_z_%d" % b)
                scales = keep.tile([P, POSITIONS], U8, align_bytes=64, name="scales_z_%d" % b)
                z_mx[b] = (codes, scales)
            cols = slice(h * P, (h + 1) * P)
            nc.vector.quantize_mx(
                out=z_mx[b][0][:, cols].bitcast(FP8X4),
                scales=z_mx[b][1][:, cols],
                in_=z_grouped[b][:, h * P * PACK : (h + 1) * P * PACK],
            )

        def fuse(b):
            every = slice(0, POSITIONS)
            fused[b] = fused_banks.tile([P, POSITIONS], F32, name="fused")
            multiply(nc, fused[b][:], wf_mx[0], slice(P, 2 * P), x_mx[b], every, True, False)
            multiply(nc, fused[b][:], wf_mx[0], slice(0, P), z_mx[b], every, False, True)

        def fuse_x_half(b, h):
            cols = slice(h * P, (h + 1) * P)
            fused[b, h] = fused_banks.tile([P, P], F32, name="fused")
            multiply(nc, fused[b, h][:], wf_mx[0], slice(P, 2 * P), x_mx[b], cols, True, False)

        def fuse_z_half(b, h):
            cols = slice(h * P, (h + 1) * P)
            multiply(nc, fused[b, h][:], wf_mx[0], slice(0, P), z_mx[b], cols, False, True)

        def add_bias_and_store(b):
            result = keep.tile([P, POSITIONS], F32, name="result_%d" % b)
            nc.scalar.activation(out=result[:], in_=fused[b][:], func=ACT.Identity, bias=small[:, 0:1])
            nc.sync.dma_start(out=out[b], in_=result[:])

        def add_bias_and_store_half(b, h):
            result = keep.tile([P, P], F32, name="result_%d%d" % (b, h))
            nc.scalar.activation(out=result[:], in_=fused[b, h][:], func=ACT.Identity, bias=small[:, 0:1])
            nc.sync.dma_start(out=out[b, :, h * P : (h + 1) * P], in_=result[:])

        def add_bias_on_vector_and_store_half(b, h):
            result = keep.tile([P, P], F32, name="result_%d%d" % (b, h))
            nc.vector.tensor_scalar_add(out=result[:], in0=fused[b, h][:], scalar1=small[:, 0:1])
            nc.sync.dma_start(out=out[b, :, h * P : (h + 1) * P], in_=result[:])

        def spread_small():
            spread = small_bank.tile([P, SPREAD_COLS], F32, name="spread")
            nc.tensor.matmul(out=spread[:], lhsT=small_rows[:], rhs=small_picks[:], start=True, stop=True)
            nc.scalar.copy(out=small[:], in_=spread[:, 0 : GAMMA_COL + 1])

        def flip_wf():
            wf_flipped.append(flip_k_last(nc, banks, ident, wf_sb))

        def leave_wf():
            wf_grouped.append(leave_psum(nc, keep, wf_flipped[0], "wf"))

        def quantise_wf():
            wf_mx.append(quantise(nc, keep, wf_grouped[0], "wf"))

        flip_attention(0, 0)
        flip_attention(0, 1)
        group_v(0)
        quantise_attention(0, 0)
        quantise_v(0)
        quantise_attention(0, 1)
        flip_attention(1, 0)
        flip_attention(1, 1)
        spread_small()
        mix(0)
        group_v(1)
        quantise_attention(1, 0)
        quantise_v(1)
        quantise_attention(1, 1)
        flip_wf()
        mix(1)
        group_x(0)
        leave_wf()
        group_x(1)
        add_v(0, 0)
        add_v(0, 1)
        quantise_x(0)
        quantise_z(0)
        quantise_wf()
        fuse(0)
        add_v(1, 0)
        add_v(1, 1)
        quantise_x(1)
        fuse_x_half(1, 0)
        fuse_x_half(1, 1)
        quantise_z_half(1, 0)
        quantise_z_half(1, 1)
        add_bias_and_store(0)
        fuse_z_half(1, 0)
        add_bias_and_store_half(1, 0)
        fuse_z_half(1, 1)
        add_bias_and_store_half(1, 1)
